import numpy as np
import ml_dtypes


def mxq(x, axis, fmt="e4m3"):
    dtype, down = {"e4m3": (ml_dtypes.float8_e4m3fn, 7), "e5m2": (ml_dtypes.float8_e5m2, 14)}[fmt]
    v = np.moveaxis(np.asarray(x, np.float32).astype(ml_dtypes.bfloat16).astype(np.float64), axis, -1)
    blocks = v.reshape(v.shape[:-1] + (-1, 32))
    amax = np.abs(blocks).max(-1, keepdims=True)
    byte = np.maximum(np.where(amax > 0, np.frexp(amax)[1] - 1 + 127, 0) - down, 1)
    scale = np.exp2(byte - 127.0)
    codes = (blocks / scale).astype(np.float32).astype(dtype).astype(np.float64)
    return np.moveaxis((codes * scale).reshape(v.shape), -1, axis)


WIDE = False


def mx_kscale(k):
    if not WIDE:
        return np.ones(k)
    levels = np.array([10, -10, 5, -5, 0])
    a = np.random.permutation(np.resize(levels, k // 512 * 4)).reshape(k // 512, 4)
    idx = np.arange(k)
    return np.exp2(a[idx // 512, idx % 128 // 32])


BF16 = ml_dtypes.bfloat16


def bf(x):
    return np.asarray(x, np.float32).astype(BF16)


def f64(x):
    return np.asarray(x).astype(np.float64)


E2M1 = np.array([0.0, 0.5, 1.0, 1.5, 2.0, 3.0, 4.0, 6.0, -0.0, -0.5, -1.0, -1.5, -2.0, -3.0, -4.0, -6.0])


def pack_weight(w, fmt):
    k, n = w.shape
    w = f64(bf(w)).reshape(k // 32, 32, n)
    amax = np.abs(w).max(1)
    if fmt == "e4m3":
        byte = np.frexp(amax)[1] - 1 + 127 - 7
    else:
        mant, ex = np.frexp(amax / 6.0)
        byte = np.where(mant > 0.5, ex, ex - 1) + 127
    byte = np.clip(np.where(amax > 0, byte, 1), 1, 254)
    scaled = (w * np.exp2(127.0 - byte)[:, None, :]).reshape(k, n).astype(np.float32)
    by_word = np.ascontiguousarray(scaled.reshape(k // 512, 128, 4, n).transpose(0, 1, 3, 2))
    if fmt == "e4m3":
        words = by_word.astype(ml_dtypes.float8_e4m3fn).view(np.uint8)
    else:
        c = by_word.astype(ml_dtypes.float4_e2m1fn).view(np.uint8) & 0xF
        words = c[..., 0::2] | (c[..., 1::2] << 4)
    return np.ascontiguousarray(words), np.ascontiguousarray(byte.astype(np.uint8).reshape(k // 512, 16, n))


def unpack_weight(words, scales, fmt):
    g, p, n, _ = words.shape
    if fmt == "e4m3":
        vals = np.ascontiguousarray(words).view(ml_dtypes.float8_e4m3fn).astype(np.float64)
    else:
        nib = np.empty((g, p, n, 4), np.uint8)
        nib[..., 0::2] = words & 0xF
        nib[..., 1::2] = words >> 4
        vals = E2M1[nib]
    vals = vals * np.repeat(np.exp2(scales.astype(np.float64) - 127.0), 8, axis=1)[..., None]
    return vals.transpose(0, 1, 3, 2).reshape(g * 512, n)


B, D, C, NP, NS = 1024, 2048, 512, 512, 512
ALPHA_NEG = 1.0 / 10.0
FMT = "e4m3"


def relu(v):
    return np.maximum(v, 0.0)


def setup_inputs():
    t = mx_kscale(NP)
    u = mx_kscale(NS)
    x_batch = bf(np.random.uniform(size=(B, D)))
    predicted = bf(np.random.standard_normal((B, D)))
    r_som = bf(np.maximum(np.random.standard_normal((B, NS)), 0.0) * 1.1 * u)
    r_neg_batch = bf(np.random.uniform(size=(B, D)) * 0.5)
    w_ff = np.random.standard_normal((NP, D)) * 1.5 / np.sqrt(D) * t[:, None]
    w_inh = np.random.standard_normal((D, NP)) * 1.2 / np.sqrt(NP) / t
    w_som = np.random.standard_normal((D, NS)) * 0.9 / np.sqrt(NS) / u
    ff_words, ff_scales = pack_weight(np.ascontiguousarray(w_ff.T), FMT)
    inh_words, inh_scales = pack_weight(np.ascontiguousarray(w_inh.T), FMT)
    som_words, som_scales = pack_weight(np.ascontiguousarray(w_som.T), FMT)
    return {
        "x_batch": x_batch,
        "predicted": predicted,
        "r_som": r_som,
        "r_neg_batch": r_neg_batch,
        "W_pv1_ff_words": ff_words,
        "W_pv1_ff_scales": ff_scales,
        "W_inh_pe_neg_words": inh_words,
        "W_inh_pe_neg_scales": inh_scales,
        "W_som_dend_words": som_words,
        "W_som_dend_scales": som_scales,
    }


def reference(x_batch, predicted, r_som, r_neg_batch, W_pv1_ff_words, W_pv1_ff_scales, W_inh_pe_neg_words, W_inh_pe_neg_scales, W_som_dend_words, W_som_dend_scales):
    xf, pf = f64(x_batch), f64(predicted)
    r_pv1 = relu(mxq(xf, 1, "e4m3") @ unpack_weight(W_pv1_ff_words, W_pv1_ff_scales, FMT))
    inh_pv = mxq(r_pv1, 1, "e4m3") @ unpack_weight(W_inh_pe_neg_words, W_inh_pe_neg_scales, FMT)
    inh_som = mxq(f64(r_som), 1, "e4m3") @ unpack_weight(W_som_dend_words, W_som_dend_scales, FMT)
    pe_neg = relu(pf - xf - inh_pv - inh_som)
    return (1.0 - ALPHA_NEG) * f64(r_neg_batch) + ALPHA_NEG * pe_neg

@@ -1,0 +1,300 @@
+from contextlib import ExitStack
+
+import concourse.mybir as mybir
+from concourse.masks import make_identity
+
+F32 = mybir.dt.float32
+BF16 = mybir.dt.bfloat16
+I32 = mybir.dt.int32
+U32 = mybir.dt.uint32
+U8 = mybir.dt.uint8
+FP8X4 = mybir.dt.float8_e4m3fn_x4
+ALU = mybir.AluOpType
+ACT = mybir.ActivationFunctionType
+
+P = 128
+PACK = 4
+K_PASS = P * PACK
+BATCH, D_MODEL, N_PV, N_SOM = 1024, 2048, 512, 512
+TILES = BATCH // P
+FF_PASSES = D_MODEL // K_PASS
+BANK = 512
+BLOCKS = D_MODEL // BANK
+HALF = D_MODEL // 2
+ALPHA = 0.1
+
+FLOPS = 2 * BATCH * (D_MODEL * N_PV + N_PV * D_MODEL + N_SOM * D_MODEL)
+
+
+def tile_pecircuits_pb_kernel(
+    tc,
+    x_batch,
+    predicted,
+    r_som,
+    r_neg_batch,
+    w_ff_words,
+    w_ff_scales,
+    w_inh_words,
+    w_inh_scales,
+    w_som_words,
+    w_som_scales,
+    out,
+):
+    nc = tc.nc
+
+    x_view = x_batch.rearrange("(p t) d -> p t d", t=TILES)
+    pred_view = predicted.rearrange("(p t) d -> p t d", t=TILES)
+    rneg_view = r_neg_batch.rearrange("(p t) d -> p t d", t=TILES)
+    rsom_view = r_som.rearrange("(p t) k -> p t k", t=TILES)
+    out_view = out.rearrange("(p t) d -> p t d", t=TILES)
+
+    with ExitStack() as ctx:
+        const = ctx.enter_context(tc.tile_pool(name="const", bufs=1))
+        inputs = ctx.enter_context(tc.tile_pool(name="inputs", bufs=1))
+        stage = ctx.enter_context(tc.tile_pool(name="stage", bufs=2))
+        quant = ctx.enter_context(tc.tile_pool(name="quant", bufs=3))
+        work = ctx.enter_context(tc.tile_pool(name="work", bufs=6))
+        psum = ctx.enter_context(tc.psum_pool(name="psum", bufs=1))
+        ctx.enter_context(tc.manual_schedule())
+
+        identity = const.tile([P, P], F32)
+        make_identity(nc, identity[:])
+
+        FF, INH, SOM = 0, 1, 2
+        planes = const.tile([P, 3, BANK], U8, align_bytes=64)
+        nc.vector.memset(planes[:].rearrange("p w n -> p (w n)").bitcast(I32), 0)
+
+        def load_planes(slab, four_planes):
+            for quadrant in range(4):
+                nc.sync.dma_start(
+                    out=planes[32 * quadrant : 32 * quadrant + 16, slab, :].bitcast(I32),
+                    in_=four_planes(quadrant),
+                )
+
+        def ff_plane_rows(quadrant):
+            return w_ff_scales[:, 4 * quadrant : 4 * quadrant + 4, :].bitcast(I32)
+
+        def inh_plane_rows(quadrant):
+            rows = w_inh_scales[0, 4 * quadrant : 4 * quadrant + 4, :].bitcast(I32)
+            return rows.rearrange("r (j n) -> j r n", j=BLOCKS)
+
+        def som_plane_rows(quadrant):
+            rows = w_som_scales[0, 4 * quadrant : 4 * quadrant + 4, :].bitcast(I32)
+            return rows.rearrange("r (j n) -> j r n", j=BLOCKS)
+
+        ff_words = const.tile([P, FF_PASSES, N_PV], U32, align_bytes=64)
+        inh_words = const.tile([P, D_MODEL], U32, align_bytes=64)
+        som_words = const.tile([P, D_MODEL], U32, align_bytes=64)
+        inh_dram = w_inh_words[0].rearrange("p n t -> p (n t)").bitcast(I32)
+        som_dram = w_som_words[0].rearrange("p n t -> p (n t)").bitcast(I32)
+
+        def block(j):
+            return slice(j * BANK, (j + 1) * BANK)
+
+        def half(h):
+            return slice(h * HALF, (h + 1) * HALF)
+
+        x_sb, pred_sb, rneg_sb, rsom_sb = {}, {}, {}, {}
+
+        def load_x_and_prediction(t):
+            x_sb[t] = inputs.tile([P, D_MODEL], BF16, name="x%d" % t)
+            nc.sync.dma_start(out=x_sb[t][:], in_=x_view[:, t, :])
+            pred_sb[t] = inputs.tile([P, D_MODEL], BF16, name="pred%d" % t)
+            nc.sync.dma_start(out=pred_sb[t][:], in_=pred_view[:, t, :])
+
+        def load_rneg(t):
+            rneg_sb[t] = inputs.tile([P, D_MODEL], BF16, name="rneg%d" % t)
+            nc.sync.dma_start(out=rneg_sb[t][:], in_=rneg_view[:, t, :])
+
+        def load_rsom(first, count):
+            tiles = inputs.tile([P, count, N_SOM], BF16, name="rsom%d" % first)
+            nc.sync.dma_start(out=tiles[:], in_=rsom_view[:, first : first + count, :])
+            for t in range(first, first + count):
+                rsom_sb[t] = tiles[:, t - first, :]
+
+        load_x_and_prediction(0)
+        load_planes(FF, ff_plane_rows)
+        for g in range(FF_PASSES):
+            nc.sync.dma_start(
+                out=ff_words[:, g, :].bitcast(I32),
+                in_=w_ff_words[g].rearrange("p n t -> p (n t)").bitcast(I32),
+            )
+        load_rsom(0, TILES // 2)
+        load_x_and_prediction(1)
+        load_planes(INH, inh_plane_rows)
+        load_planes(SOM, som_plane_rows)
+        for j in range(BLOCKS):
+            nc.sync.dma_start(out=inh_words[:, block(j)].bitcast(I32), in_=inh_dram[:, block(j)])
+            nc.sync.dma_start(out=som_words[:, block(j)].bitcast(I32), in_=som_dram[:, block(j)])
+        for t in range(TILES):
+            if t + 2 < TILES:
+                load_x_and_prediction(t + 2)
+            if t + 2 == TILES // 2:
+                load_rsom(TILES // 2, TILES // 2)
+            load_rneg(t)
+
+        x_planes, x_grouped, x_codes, x_scales = {}, {}, {}, {}
+        pv_sum, pv_sorted, act_planes, act_grouped, act_codes, act_scales = {}, {}, {}, {}, {}, {}
+        inhibition, result = {}, {}
+        PV, SOM_ACT = 0, 1
+
+        def transpose_x(t):
+            words = x_sb[t][:].bitcast(F32)
+            for bank in range(2):
+                x_planes[t, bank] = psum.tile([P, 2, 2, P], F32, name="xT%d_%d" % (t, bank), tag="xT", bufs=2)
+                for g2 in range(2):
+                    first = (2 * bank + g2) * (K_PASS // 2)
+                    for u in range(2):
+                        nc.tensor.transpose(
+                            x_planes[t, bank][:, g2, u, :],
+                            words[:, first + u : first + K_PASS // 2 : 2],
+                            identity[:],
+                        )
+
+        def group_x(t):
+            x_grouped[t] = stage.tile([P, FF_PASSES, P, PACK], BF16, name="xg%d" % t, tag="xg", align_bytes=64)
+            for bank in range(2):
+                nc.scalar.copy(
+                    out=x_grouped[t][:, 2 * bank : 2 * bank + 2, :, :].bitcast(F32),
+                    in_=x_planes[t, bank][:].rearrange("q g u b -> q g b u"),
+                )
+
+        def quantise_x(t):
+            x_codes[t] = quant.tile([P, FF_PASSES, P], U32, name="xc%d" % t, tag="xc", align_bytes=64)
+            x_scales[t] = quant.tile([P, FF_PASSES, P], U8, name="xs%d" % t, tag="xs", align_bytes=64)
+            nc.vector.quantize_mx(
+                out=x_codes[t][:].rearrange("q g b -> q (g b)").bitcast(FP8X4),
+                scales=x_scales[t][:].rearrange("q g b -> q (g b)"),
+                in_=x_grouped[t][:].rearrange("q g b k -> q (g b k)"),
+            )
+
+        def first_product(t):
+            pv_sum[t] = psum.tile([P, N_PV], F32, name="pv%d" % t, tag="pv", bufs=1)
+            for g in range(FF_PASSES):
+                nc.tensor.matmul_mx(
+                    out=pv_sum[t][:],
+                    lhsT=x_codes[t][:, g, :].bitcast(FP8X4),
+                    lhsT_scale=x_scales[t][:, g, :],
+                    rhs=ff_words[:, g, :].bitcast(FP8X4),
+                    rhs_scale=planes[4 * g : P, FF, :],
+                    start=(g == 0),
+                    stop=(g == FF_PASSES - 1),
+                )
+
+        def relu_pv(t):
+            pv_sorted[t] = stage.tile([P, 2, P, 2], BF16, name="pvs%d" % t, tag="pvs")
+            nc.scalar.activation(
+                out=pv_sorted[t][:],
+                in_=pv_sum[t][:].rearrange("b (q u e) -> b u q e", u=2, e=2),
+                func=ACT.Relu,
+            )
+
+        def transpose_activities(t):
+            act_planes[t] = psum.tile([P, 2, 2, P], F32, name="aT%d" % t, tag="aT", bufs=1)
+            pv_words = pv_sorted[t][:].rearrange("b u q e -> b (u q e)").bitcast(F32)
+            som_act_words = rsom_sb[t].bitcast(F32)
+            for u in range(2):
+                nc.tensor.transpose(act_planes[t][:, PV, u, :], pv_words[:, u * P : (u + 1) * P], identity[:])
+            for u in range(2):
+                nc.tensor.transpose(act_planes[t][:, SOM_ACT, u, :], som_act_words[:, u : K_PASS // 2 : 2], identity[:])
+
+        def group_activities(t):
+            act_grouped[t] = stage.tile([P, 2, P, PACK], BF16, name="ag%d" % t, tag="ag", align_bytes=64)
+            nc.scalar.copy(
+                out=act_grouped[t][:].bitcast(F32),
+                in_=act_planes[t][:].rearrange("q a u b -> q a b u"),
+            )
+
+        def quantise_activities(t):
+            act_codes[t] = quant.tile([P, 2, P], U32, name="ac%d" % t, tag="ac", align_bytes=64)
+            act_scales[t] = quant.tile([P, 2, P], U8, name="as%d" % t, tag="as", align_bytes=64)
+            nc.vector.quantize_mx(
+                out=act_codes[t][:].rearrange("q a b -> q (a b)").bitcast(FP8X4),
+                scales=act_scales[t][:].rearrange("q a b -> q (a b)"),
+                in_=act_grouped[t][:].rearrange("q a b k -> q (a b k)"),
+            )
+
+        def second_products(t):
+            for j in range(BLOCKS):
+                inhibition[t, j] = psum.tile([P, BANK], F32, name="inh%d_%d" % (t, j), tag="inh", bufs=4)
+                nc.tensor.matmul_mx(
+                    out=inhibition[t, j][:],
+                    lhsT=act_codes[t][:, PV, :].bitcast(FP8X4),
+                    lhsT_scale=act_scales[t][:, PV, :],
+                    rhs=inh_words[:, block(j)].bitcast(FP8X4),
+                    rhs_scale=planes[4 * j : P, INH, :],
+                    start=True,
+                    stop=False,
+                )
+                nc.tensor.matmul_mx(
+                    out=inhibition[t, j][:],
+                    lhsT=act_codes[t][:, SOM_ACT, :].bitcast(FP8X4),
+                    lhsT_scale=act_scales[t][:, SOM_ACT, :],
+                    rhs=som_words[:, block(j)].bitcast(FP8X4),
+                    rhs_scale=planes[4 * j : P, SOM, :],
+                    start=False,
+                    stop=True,
+                )
+
+        def difference(t, h):
+            if h == 0:
+                result[t] = work.tile([P, D_MODEL], F32, name="res%d" % t, tag="res")
+            nc.vector.tensor_tensor(
+                out=result[t][:, half(h)], in0=pred_sb[t][:, half(h)], in1=x_sb[t][:, half(h)], op=ALU.subtract
+            )
+
+        def subtract_inhibition(t, j):
+            nc.vector.tensor_tensor(
+                out=result[t][:, block(j)], in0=result[t][:, block(j)], in1=inhibition[t, j][:], op=ALU.subtract
+            )
+
+        def scaled_relu(t, h):
+            nc.scalar.activation(out=result[t][:, half(h)], in_=result[t][:, half(h)], func=ACT.Relu, scale=ALPHA)
+
+        def filter_and_store(t, h):
+            nc.vector.scalar_tensor_tensor(
+                out=result[t][:, half(h)],
+                in0=rneg_sb[t][:, half(h)],
+                scalar=1.0 - ALPHA,
+                in1=result[t][:, half(h)],
+                op0=ALU.mult,
+                op1=ALU.add,
+            )
+            nc.sync.dma_start(out=out_view[:, t, half(h)], in_=result[t][:, half(h)])
+
+        def live(t):
+            return 0 <= t < TILES
+
+        for i in range(-2, TILES):
+            if live(i + 1):
+                quantise_x(i + 1)
+            if live(i):
+                second_products(i)
+            if live(i + 1):
+                first_product(i + 1)
+            if live(i):
+                subtract_inhibition(i, 0)
+                subtract_inhibition(i, 1)
+                scaled_relu(i, 0)
+            if live(i + 1):
+                relu_pv(i + 1)
+            if live(i):
+                subtract_inhibition(i, 2)
+                subtract_inhibition(i, 3)
+                scaled_relu(i, 1)
+            if live(i + 2):
+                transpose_x(i + 2)
+            if live(i + 1):
+                transpose_activities(i + 1)
+                group_activities(i + 1)
+            if live(i + 2):
+                group_x(i + 2)
+                difference(i + 2, 0)
+            if live(i):
+                filter_and_store(i, 0)
+            if live(i + 1):
+                quantise_activities(i + 1)
+            if live(i):
+                filter_and_store(i, 1)
+            if live(i + 2):
+                difference(i + 2, 1)

@@ -22,6 +22,8 @@ BANK = 512
 BLOCKS = D_MODEL // BANK
 HALF = D_MODEL // 2
 ALPHA = 0.1
+GPSIMD_BLOCKS = 2
+HEAD_TILES = 2
 
 FLOPS = 2 * BATCH * (D_MODEL * N_PV + N_PV * D_MODEL + N_SOM * D_MODEL)
 
@@ -112,6 +114,10 @@ def tile_pecircuits_pb_kernel(
             for t in range(first, first + count):
                 rsom_sb[t] = tiles[:, t - first, :]
 
+        def load_second_stage_words(j):
+            nc.sync.dma_start(out=inh_words[:, block(j)].bitcast(I32), in_=inh_dram[:, block(j)])
+            nc.sync.dma_start(out=som_words[:, block(j)].bitcast(I32), in_=som_dram[:, block(j)])
+
         load_x_and_prediction(0)
         load_planes(FF, ff_plane_rows)
         for g in range(FF_PASSES):
@@ -119,19 +125,20 @@ def tile_pecircuits_pb_kernel(
                 out=ff_words[:, g, :].bitcast(I32),
                 in_=w_ff_words[g].rearrange("p n t -> p (n t)").bitcast(I32),
             )
-        load_rsom(0, TILES // 2)
+        load_rsom(0, HEAD_TILES)
         load_x_and_prediction(1)
         load_planes(INH, inh_plane_rows)
         load_planes(SOM, som_plane_rows)
-        for j in range(BLOCKS):
-            nc.sync.dma_start(out=inh_words[:, block(j)].bitcast(I32), in_=inh_dram[:, block(j)])
-            nc.sync.dma_start(out=som_words[:, block(j)].bitcast(I32), in_=som_dram[:, block(j)])
-        for t in range(TILES):
-            if t + 2 < TILES:
-                load_x_and_prediction(t + 2)
-            if t + 2 == TILES // 2:
-                load_rsom(TILES // 2, TILES // 2)
-            load_rneg(t)
+        load_second_stage_words(0)
+        load_second_stage_words(1)
+        load_rneg(0)
+        load_second_stage_words(2)
+        load_second_stage_words(3)
+        load_rsom(HEAD_TILES, TILES - HEAD_TILES)
+        for t in range(2, TILES):
+            load_x_and_prediction(t)
+            load_rneg(t - 1)
+        load_rneg(TILES - 1)
 
         x_planes, x_grouped, x_codes, x_scales = {}, {}, {}, {}
         pv_sum, pv_sorted, act_planes, act_grouped, act_codes, act_scales = {}, {}, {}, {}, {}, {}
@@ -236,11 +243,12 @@ def tile_pecircuits_pb_kernel(
                     stop=True,
                 )
 
-        def difference(t, h):
-            if h == 0:
+        def difference(t, j):
+            if j == 0:
                 result[t] = work.tile([P, D_MODEL], F32, name="res%d" % t, tag="res")
-            nc.vector.tensor_tensor(
-                out=result[t][:, half(h)], in0=pred_sb[t][:, half(h)], in1=x_sb[t][:, half(h)], op=ALU.subtract
+            engine = nc.gpsimd if (t >= HEAD_TILES and j < GPSIMD_BLOCKS) else nc.vector
+            engine.tensor_tensor(
+                out=result[t][:, block(j)], in0=pred_sb[t][:, block(j)], in1=x_sb[t][:, block(j)], op=ALU.subtract
             )
 
         def subtract_inhibition(t, j):
@@ -248,8 +256,8 @@ def tile_pecircuits_pb_kernel(
                 out=result[t][:, block(j)], in0=result[t][:, block(j)], in1=inhibition[t, j][:], op=ALU.subtract
             )
 
-        def scaled_relu(t, h):
-            nc.scalar.activation(out=result[t][:, half(h)], in_=result[t][:, half(h)], func=ACT.Relu, scale=ALPHA)
+        def scaled_relu(t, j):
+            nc.scalar.activation(out=result[t][:, block(j)], in_=result[t][:, block(j)], func=ACT.Relu, scale=ALPHA)
 
         def filter_and_store(t, h):
             nc.vector.scalar_tensor_tensor(
@@ -273,28 +281,27 @@ def tile_pecircuits_pb_kernel(
             if live(i + 1):
                 first_product(i + 1)
             if live(i):
-                subtract_inhibition(i, 0)
-                subtract_inhibition(i, 1)
-                scaled_relu(i, 0)
+                for j in range(BLOCKS):
+                    subtract_inhibition(i, j)
+                    scaled_relu(i, j)
             if live(i + 1):
                 relu_pv(i + 1)
-            if live(i):
-                subtract_inhibition(i, 2)
-                subtract_inhibition(i, 3)
-                scaled_relu(i, 1)
             if live(i + 2):
                 transpose_x(i + 2)
             if live(i + 1):
                 transpose_activities(i + 1)
-                group_activities(i + 1)
             if live(i + 2):
                 group_x(i + 2)
-                difference(i + 2, 0)
+            if live(i + 1):
+                group_activities(i + 1)
             if live(i):
                 filter_and_store(i, 0)
-            if live(i + 1):
-                quantise_activities(i + 1)
-            if live(i):
                 filter_and_store(i, 1)
             if live(i + 2):
+                difference(i + 2, 0)
                 difference(i + 2, 1)
+            if live(i + 1):
+                quantise_activities(i + 1)
+            if live(i + 2):
+                difference(i + 2, 2)
+                difference(i + 2, 3)

@@ -22,7 +22,7 @@ BANK = 512
 BLOCKS = D_MODEL // BANK
 HALF = D_MODEL // 2
 ALPHA = 0.1
-GPSIMD_BLOCKS = 2
+TENSOR_BLOCKS = 2
 HEAD_TILES = 2
 
 FLOPS = 2 * BATCH * (D_MODEL * N_PV + N_PV * D_MODEL + N_SOM * D_MODEL)
@@ -55,16 +55,20 @@ def tile_pecircuits_pb_kernel(
         inputs = ctx.enter_context(tc.tile_pool(name="inputs", bufs=1))
         stage = ctx.enter_context(tc.tile_pool(name="stage", bufs=2))
         quant = ctx.enter_context(tc.tile_pool(name="quant", bufs=3))
-        work = ctx.enter_context(tc.tile_pool(name="work", bufs=6))
+        work = ctx.enter_context(tc.tile_pool(name="work", bufs=7))
         psum = ctx.enter_context(tc.psum_pool(name="psum", bufs=1))
         ctx.enter_context(tc.manual_schedule())
 
         identity = const.tile([P, P], F32)
         make_identity(nc, identity[:])
+        plus_identity = const.tile([P, P], BF16)
+        make_identity(nc, plus_identity[:])
 
         FF, INH, SOM = 0, 1, 2
         planes = const.tile([P, 3, BANK], U8, align_bytes=64)
         nc.vector.memset(planes[:].rearrange("p w n -> p (w n)").bitcast(I32), 0)
+        minus_identity = const.tile([P, P], BF16)
+        nc.vector.tensor_scalar_mul(minus_identity[:], plus_identity[:], -1.0)
 
         def load_planes(slab, four_planes):
             for quadrant in range(4):
@@ -98,9 +102,11 @@ def tile_pecircuits_pb_kernel(
 
         x_sb, pred_sb, rneg_sb, rsom_sb = {}, {}, {}, {}
 
-        def load_x_and_prediction(t):
+        def load_x(t):
             x_sb[t] = inputs.tile([P, D_MODEL], BF16, name="x%d" % t)
             nc.sync.dma_start(out=x_sb[t][:], in_=x_view[:, t, :])
+
+        def load_prediction(t):
             pred_sb[t] = inputs.tile([P, D_MODEL], BF16, name="pred%d" % t)
             nc.sync.dma_start(out=pred_sb[t][:], in_=pred_view[:, t, :])
 
@@ -114,31 +120,37 @@ def tile_pecircuits_pb_kernel(
             for t in range(first, first + count):
                 rsom_sb[t] = tiles[:, t - first, :]
 
-        def load_second_stage_words(j):
-            nc.sync.dma_start(out=inh_words[:, block(j)].bitcast(I32), in_=inh_dram[:, block(j)])
-            nc.sync.dma_start(out=som_words[:, block(j)].bitcast(I32), in_=som_dram[:, block(j)])
-
-        load_x_and_prediction(0)
-        load_planes(FF, ff_plane_rows)
-        for g in range(FF_PASSES):
+        def load_first_stage_words(h):
             nc.sync.dma_start(
-                out=ff_words[:, g, :].bitcast(I32),
-                in_=w_ff_words[g].rearrange("p n t -> p (n t)").bitcast(I32),
+                out=ff_words[:, 2 * h : 2 * h + 2, :].bitcast(I32),
+                in_=w_ff_words[2 * h : 2 * h + 2].rearrange("g p n t -> p g (n t)").bitcast(I32),
             )
-        load_rsom(0, HEAD_TILES)
-        load_x_and_prediction(1)
+
+        load_x(0)
+        load_planes(FF, ff_plane_rows)
+        load_first_stage_words(0)
+        load_first_stage_words(1)
+        load_x(1)
+        load_x(2)
         load_planes(INH, inh_plane_rows)
+        load_rsom(0, TILES // 2)
+        load_prediction(0)
+        nc.sync.dma_start(out=inh_words[:, half(0)].bitcast(I32), in_=inh_dram[:, half(0)])
         load_planes(SOM, som_plane_rows)
-        load_second_stage_words(0)
-        load_second_stage_words(1)
+        nc.sync.dma_start(out=som_words[:, half(0)].bitcast(I32), in_=som_dram[:, half(0)])
+        nc.sync.dma_start(out=inh_words[:, half(1)].bitcast(I32), in_=inh_dram[:, half(1)])
+        nc.sync.dma_start(out=som_words[:, half(1)].bitcast(I32), in_=som_dram[:, half(1)])
         load_rneg(0)
-        load_second_stage_words(2)
-        load_second_stage_words(3)
-        load_rsom(HEAD_TILES, TILES - HEAD_TILES)
-        for t in range(2, TILES):
-            load_x_and_prediction(t)
-            load_rneg(t - 1)
-        load_rneg(TILES - 1)
+        load_prediction(1)
+        load_x(3)
+        for i in range(1, TILES):
+            if i + 3 < TILES:
+                load_x(i + 3)
+            if i == 1:
+                load_rsom(TILES // 2, TILES // 2)
+            load_rneg(i)
+            if i + 1 < TILES:
+                load_prediction(i + 1)
 
         x_planes, x_grouped, x_codes, x_scales = {}, {}, {}, {}
         pv_sum, pv_sorted, act_planes, act_grouped, act_codes, act_scales = {}, {}, {}, {}, {}, {}
@@ -148,7 +160,7 @@ def tile_pecircuits_pb_kernel(
         def transpose_x(t):
             words = x_sb[t][:].bitcast(F32)
             for bank in range(2):
-                x_planes[t, bank] = psum.tile([P, 2, 2, P], F32, name="xT%d_%d" % (t, bank), tag="xT", bufs=2)
+                x_planes[t, bank] = psum.tile([P, 2, 2, P], F32, name="xT%d_%d" % (t, bank), tag="short", bufs=4)
                 for g2 in range(2):
                     first = (2 * bank + g2) * (K_PASS // 2)
                     for u in range(2):
@@ -159,7 +171,7 @@ def tile_pecircuits_pb_kernel(
                         )
 
         def group_x(t):
-            x_grouped[t] = stage.tile([P, FF_PASSES, P, PACK], BF16, name="xg%d" % t, tag="xg", align_bytes=64)
+            x_grouped[t] = stage.tile([P, FF_PASSES, P, PACK], BF16, name="xg%d" % t, tag="xg", bufs=3, align_bytes=64)
             for bank in range(2):
                 nc.scalar.copy(
                     out=x_grouped[t][:, 2 * bank : 2 * bank + 2, :, :].bitcast(F32),
@@ -176,7 +188,7 @@ def tile_pecircuits_pb_kernel(
             )
 
         def first_product(t):
-            pv_sum[t] = psum.tile([P, N_PV], F32, name="pv%d" % t, tag="pv", bufs=1)
+            pv_sum[t] = psum.tile([P, N_PV], F32, name="pv%d" % t, tag="short", bufs=4)
             for g in range(FF_PASSES):
                 nc.tensor.matmul_mx(
                     out=pv_sum[t][:],
@@ -197,7 +209,7 @@ def tile_pecircuits_pb_kernel(
             )
 
         def transpose_activities(t):
-            act_planes[t] = psum.tile([P, 2, 2, P], F32, name="aT%d" % t, tag="aT", bufs=1)
+            act_planes[t] = psum.tile([P, 2, 2, P], F32, name="aT%d" % t, tag="short", bufs=4)
             pv_words = pv_sorted[t][:].rearrange("b u q e -> b (u q e)").bitcast(F32)
             som_act_words = rsom_sb[t].bitcast(F32)
             for u in range(2):
@@ -243,13 +255,20 @@ def tile_pecircuits_pb_kernel(
                     stop=True,
                 )
 
-        def difference(t, j):
-            if j == 0:
-                result[t] = work.tile([P, D_MODEL], F32, name="res%d" % t, tag="res")
-            engine = nc.gpsimd if (t >= HEAD_TILES and j < GPSIMD_BLOCKS) else nc.vector
-            engine.tensor_tensor(
-                out=result[t][:, block(j)], in0=pred_sb[t][:, block(j)], in1=x_sb[t][:, block(j)], op=ALU.subtract
-            )
+        def tensor_blocks(t):
+            return 0 if t < HEAD_TILES else TENSOR_BLOCKS
+
+        def difference_on_tensor(t):
+            result[t] = work.tile([P, D_MODEL], F32, name="res%d" % t, tag="res")
+            for j in range(tensor_blocks(t)):
+                diff = psum.tile([P, BANK], F32, name="diff%d_%d" % (t, j), tag="short", bufs=4)
+                nc.tensor.matmul(out=diff[:], lhsT=plus_identity[:], rhs=pred_sb[t][:, block(j)], start=True, stop=False)
+                nc.tensor.matmul(out=diff[:], lhsT=minus_identity[:], rhs=x_sb[t][:, block(j)], start=False, stop=True)
+                nc.scalar.copy(out=result[t][:, block(j)], in_=diff[:])
+
+        def difference_on_vector(t):
+            rest = slice(tensor_blocks(t) * BANK, D_MODEL)
+            nc.vector.tensor_tensor(out=result[t][:, rest], in0=pred_sb[t][:, rest], in1=x_sb[t][:, rest], op=ALU.subtract)
 
         def subtract_inhibition(t, j):
             nc.vector.tensor_tensor(
@@ -273,35 +292,33 @@ def tile_pecircuits_pb_kernel(
         def live(t):
             return 0 <= t < TILES
 
-        for i in range(-2, TILES):
-            if live(i + 1):
-                quantise_x(i + 1)
+        for i in range(-3, TILES):
+            if live(i + 2):
+                quantise_x(i + 2)
             if live(i):
                 second_products(i)
-            if live(i + 1):
-                first_product(i + 1)
-            if live(i):
-                for j in range(BLOCKS):
+                for j in range(BLOCKS // 2):
                     subtract_inhibition(i, j)
                     scaled_relu(i, j)
             if live(i + 1):
-                relu_pv(i + 1)
-            if live(i + 2):
-                transpose_x(i + 2)
-            if live(i + 1):
                 transpose_activities(i + 1)
-            if live(i + 2):
-                group_x(i + 2)
-            if live(i + 1):
                 group_activities(i + 1)
             if live(i):
+                for j in range(BLOCKS // 2, BLOCKS):
+                    subtract_inhibition(i, j)
+                    scaled_relu(i, j)
                 filter_and_store(i, 0)
-                filter_and_store(i, 1)
-            if live(i + 2):
-                difference(i + 2, 0)
-                difference(i + 2, 1)
             if live(i + 1):
                 quantise_activities(i + 1)
+            if live(i):
+                filter_and_store(i, 1)
+            if live(i + 3):
+                transpose_x(i + 3)
+                group_x(i + 3)
+            if live(i + 1):
+                difference_on_tensor(i + 1)
             if live(i + 2):
-                difference(i + 2, 2)
-                difference(i + 2, 3)
+                first_product(i + 2)
+                relu_pv(i + 2)
+            if live(i + 1):
+                difference_on_vector(i + 1)

@@ -22,7 +22,8 @@ BANK = 512
 BLOCKS = D_MODEL // BANK
 HALF = D_MODEL // 2
 ALPHA = 0.1
-TENSOR_BLOCKS = 2
+TENSOR_BLOCKS = 1
+GPSIMD_BLOCKS = 2
 HEAD_TILES = 2
 
 FLOPS = 2 * BATCH * (D_MODEL * N_PV + N_PV * D_MODEL + N_SOM * D_MODEL)
@@ -255,19 +256,23 @@ def tile_pecircuits_pb_kernel(
                     stop=True,
                 )
 
-        def tensor_blocks(t):
-            return 0 if t < HEAD_TILES else TENSOR_BLOCKS
+        def helped_blocks(t, blocks):
+            return 0 if t < HEAD_TILES else blocks
 
-        def difference_on_tensor(t):
+        def difference_by_helpers(t):
             result[t] = work.tile([P, D_MODEL], F32, name="res%d" % t, tag="res")
-            for j in range(tensor_blocks(t)):
+            for j in range(helped_blocks(t, TENSOR_BLOCKS)):
                 diff = psum.tile([P, BANK], F32, name="diff%d_%d" % (t, j), tag="short", bufs=4)
                 nc.tensor.matmul(out=diff[:], lhsT=plus_identity[:], rhs=pred_sb[t][:, block(j)], start=True, stop=False)
                 nc.tensor.matmul(out=diff[:], lhsT=minus_identity[:], rhs=x_sb[t][:, block(j)], start=False, stop=True)
                 nc.scalar.copy(out=result[t][:, block(j)], in_=diff[:])
+            for j in range(helped_blocks(t, TENSOR_BLOCKS), helped_blocks(t, TENSOR_BLOCKS + GPSIMD_BLOCKS)):
+                nc.gpsimd.tensor_tensor(
+                    out=result[t][:, block(j)], in0=pred_sb[t][:, block(j)], in1=x_sb[t][:, block(j)], op=ALU.subtract
+                )
 
         def difference_on_vector(t):
-            rest = slice(tensor_blocks(t) * BANK, D_MODEL)
+            rest = slice(helped_blocks(t, TENSOR_BLOCKS + GPSIMD_BLOCKS) * BANK, D_MODEL)
             nc.vector.tensor_tensor(out=result[t][:, rest], in0=pred_sb[t][:, rest], in1=x_sb[t][:, rest], op=ALU.subtract)
 
         def subtract_inhibition(t, j):
@@ -316,7 +321,7 @@ def tile_pecircuits_pb_kernel(
                 transpose_x(i + 3)
                 group_x(i + 3)
             if live(i + 1):
-                difference_on_tensor(i + 1)
+                difference_by_helpers(i + 1)
             if live(i + 2):
                 first_product(i + 2)
                 relu_pv(i + 2)

@@ -22,9 +22,9 @@ BANK = 512
 BLOCKS = D_MODEL // BANK
 HALF = D_MODEL // 2
 ALPHA = 0.1
-TENSOR_BLOCKS = 1
-GPSIMD_BLOCKS = 2
-HEAD_TILES = 2
+SHARES = [(0, 0)] + [(1, 2), (2, 2)] * 3 + [(2, 2)]
+ERR_BUFS = 2
+OUT_BUFS = 13
 
 FLOPS = 2 * BATCH * (D_MODEL * N_PV + N_PV * D_MODEL + N_SOM * D_MODEL)
 
@@ -127,35 +127,48 @@ def tile_pecircuits_pb_kernel(
                 in_=w_ff_words[2 * h : 2 * h + 2].rearrange("g p n t -> p g (n t)").bitcast(I32),
             )
 
+        def load_words(dst, src, h):
+            nc.sync.dma_start(out=dst[:, half(h)].bitcast(I32), in_=src[:, half(h)])
+
         load_x(0)
-        load_planes(FF, ff_plane_rows)
         load_first_stage_words(0)
+        load_planes(FF, ff_plane_rows)
         load_first_stage_words(1)
         load_x(1)
+        load_rsom(0, 2)
         load_x(2)
-        load_planes(INH, inh_plane_rows)
-        load_rsom(0, TILES // 2)
         load_prediction(0)
-        nc.sync.dma_start(out=inh_words[:, half(0)].bitcast(I32), in_=inh_dram[:, half(0)])
+        load_words(som_words, som_dram, 0)
+        load_planes(INH, inh_plane_rows)
+        load_words(inh_words, inh_dram, 0)
+        load_words(som_words, som_dram, 1)
         load_planes(SOM, som_plane_rows)
-        nc.sync.dma_start(out=som_words[:, half(0)].bitcast(I32), in_=som_dram[:, half(0)])
-        nc.sync.dma_start(out=inh_words[:, half(1)].bitcast(I32), in_=inh_dram[:, half(1)])
-        nc.sync.dma_start(out=som_words[:, half(1)].bitcast(I32), in_=som_dram[:, half(1)])
-        load_rneg(0)
+        load_words(inh_words, inh_dram, 1)
         load_prediction(1)
         load_x(3)
-        for i in range(1, TILES):
-            if i + 3 < TILES:
-                load_x(i + 3)
-            if i == 1:
-                load_rsom(TILES // 2, TILES // 2)
-            load_rneg(i)
-            if i + 1 < TILES:
-                load_prediction(i + 1)
+        load_rneg(0)
+        load_prediction(2)
+        load_rsom(2, 6)
+        load_x(4)
+        load_rneg(1)
+        load_rneg(2)
+        load_prediction(3)
+        load_x(5)
+        load_rneg(3)
+        load_prediction(4)
+        load_x(6)
+        load_rneg(4)
+        load_prediction(5)
+        load_x(7)
+        load_rneg(5)
+        load_prediction(6)
+        load_rneg(6)
+        load_prediction(7)
+        load_rneg(7)
 
         x_planes, x_grouped, x_codes, x_scales = {}, {}, {}, {}
         pv_sum, pv_sorted, act_planes, act_grouped, act_codes, act_scales = {}, {}, {}, {}, {}, {}
-        inhibition, result = {}, {}
+        inhibition, error = {}, {}
         PV, SOM_ACT = 0, 1
 
         def transpose_x(t):
@@ -256,74 +269,80 @@ def tile_pecircuits_pb_kernel(
                     stop=True,
                 )
 
-        def helped_blocks(t, blocks):
-            return 0 if t < HEAD_TILES else blocks
+        def diff_shares(t):
+            return SHARES[t]
 
-        def difference_by_helpers(t):
-            result[t] = work.tile([P, D_MODEL], F32, name="res%d" % t, tag="res")
-            for j in range(helped_blocks(t, TENSOR_BLOCKS)):
+        def new_work(t):
+            for h in range(2):
+                error[t, h] = work.tile([P, HALF], F32, name="err%d_%d" % (t, h), tag="err%d" % h, bufs=ERR_BUFS)
+
+        def error_block(t, j):
+            first = (j % 2) * BANK
+            return error[t, j // 2][:, first : first + BANK]
+
+        def difference_on_tensor(t):
+            for j in range(SHARES[t][0]):
                 diff = psum.tile([P, BANK], F32, name="diff%d_%d" % (t, j), tag="short", bufs=4)
                 nc.tensor.matmul(out=diff[:], lhsT=plus_identity[:], rhs=pred_sb[t][:, block(j)], start=True, stop=False)
                 nc.tensor.matmul(out=diff[:], lhsT=minus_identity[:], rhs=x_sb[t][:, block(j)], start=False, stop=True)
-                nc.scalar.copy(out=result[t][:, block(j)], in_=diff[:])
-            for j in range(helped_blocks(t, TENSOR_BLOCKS), helped_blocks(t, TENSOR_BLOCKS + GPSIMD_BLOCKS)):
-                nc.gpsimd.tensor_tensor(
-                    out=result[t][:, block(j)], in0=pred_sb[t][:, block(j)], in1=x_sb[t][:, block(j)], op=ALU.subtract
-                )
+                nc.scalar.copy(out=error_block(t, j), in_=diff[:])
+
+        def difference_on_gpsimd(t):
+            for j in range(BLOCKS - SHARES[t][1], BLOCKS):
+                nc.gpsimd.tensor_tensor(out=error_block(t, j), in0=pred_sb[t][:, block(j)], in1=x_sb[t][:, block(j)], op=ALU.subtract)
 
         def difference_on_vector(t):
-            rest = slice(helped_blocks(t, TENSOR_BLOCKS + GPSIMD_BLOCKS) * BANK, D_MODEL)
-            nc.vector.tensor_tensor(out=result[t][:, rest], in0=pred_sb[t][:, rest], in1=x_sb[t][:, rest], op=ALU.subtract)
+            first, last = SHARES[t][0], BLOCKS - SHARES[t][1]
+            if (first, last) == (0, BLOCKS):
+                for h in range(2):
+                    nc.vector.tensor_tensor(out=error[t, h][:], in0=pred_sb[t][:, half(h)], in1=x_sb[t][:, half(h)], op=ALU.subtract)
+            else:
+                for j in range(first, last):
+                    nc.vector.tensor_tensor(out=error_block(t, j), in0=pred_sb[t][:, block(j)], in1=x_sb[t][:, block(j)], op=ALU.subtract)
 
         def subtract_inhibition(t, j):
-            nc.vector.tensor_tensor(
-                out=result[t][:, block(j)], in0=result[t][:, block(j)], in1=inhibition[t, j][:], op=ALU.subtract
-            )
+            nc.vector.tensor_tensor(out=error_block(t, j), in0=error_block(t, j), in1=inhibition[t, j][:], op=ALU.subtract)
 
         def scaled_relu(t, j):
-            nc.scalar.activation(out=result[t][:, block(j)], in_=result[t][:, block(j)], func=ACT.Relu, scale=ALPHA)
+            nc.scalar.activation(out=error_block(t, j), in_=error_block(t, j), func=ACT.Relu, scale=ALPHA)
 
         def filter_and_store(t, h):
+            filtered = work.tile([P, HALF], F32, name="out%d_%d" % (t, h), tag="out", bufs=OUT_BUFS)
             nc.vector.scalar_tensor_tensor(
-                out=result[t][:, half(h)],
-                in0=rneg_sb[t][:, half(h)],
-                scalar=1.0 - ALPHA,
-                in1=result[t][:, half(h)],
-                op0=ALU.mult,
-                op1=ALU.add,
+                out=filtered[:], in0=rneg_sb[t][:, half(h)], scalar=1.0 - ALPHA, in1=error[t, h][:], op0=ALU.mult, op1=ALU.add
             )
-            nc.sync.dma_start(out=out_view[:, t, half(h)], in_=result[t][:, half(h)])
+            nc.sync.dma_start(out=out_view[:, t, half(h)], in_=filtered[:])
 
         def live(t):
             return 0 <= t < TILES
 
-        for i in range(-3, TILES):
+        for i in range(-3, TILES + 1):
+            if live(i):
+                quantise_activities(i)
+            if live(i - 1):
+                filter_and_store(i - 1, 0)
             if live(i + 2):
                 quantise_x(i + 2)
+            if live(i - 1):
+                filter_and_store(i - 1, 1)
+            if live(i + 1):
+                new_work(i + 1)
+                difference_on_vector(i + 1)
             if live(i):
                 second_products(i)
-                for j in range(BLOCKS // 2):
-                    subtract_inhibition(i, j)
-                    scaled_relu(i, j)
             if live(i + 1):
                 transpose_activities(i + 1)
                 group_activities(i + 1)
-            if live(i):
-                for j in range(BLOCKS // 2, BLOCKS):
+                difference_on_gpsimd(i + 1)
+            for j in range(BLOCKS):
+                if live(i):
                     subtract_inhibition(i, j)
                     scaled_relu(i, j)
-                filter_and_store(i, 0)
-            if live(i + 1):
-                quantise_activities(i + 1)
-            if live(i):
-                filter_and_store(i, 1)
-            if live(i + 3):
-                transpose_x(i + 3)
-                group_x(i + 3)
-            if live(i + 1):
-                difference_by_helpers(i + 1)
+                if j == 1 and live(i + 3):
+                    transpose_x(i + 3)
+                    group_x(i + 3)
             if live(i + 2):
                 first_product(i + 2)
                 relu_pv(i + 2)
             if live(i + 1):
-                difference_on_vector(i + 1)
+                difference_on_tensor(i + 1)

@@ -24,7 +24,7 @@ HALF = D_MODEL // 2
 ALPHA = 0.1
 SHARES = [(0, 0)] + [(1, 2), (2, 2)] * 3 + [(2, 2)]
 ERR_BUFS = 2
-OUT_BUFS = 13
+OUT_BUFS = 6
 
 FLOPS = 2 * BATCH * (D_MODEL * N_PV + N_PV * D_MODEL + N_SOM * D_MODEL)
 
@@ -103,18 +103,6 @@ def tile_pecircuits_pb_kernel(
 
         x_sb, pred_sb, rneg_sb, rsom_sb = {}, {}, {}, {}
 
-        def load_x(t):
-            x_sb[t] = inputs.tile([P, D_MODEL], BF16, name="x%d" % t)
-            nc.sync.dma_start(out=x_sb[t][:], in_=x_view[:, t, :])
-
-        def load_prediction(t):
-            pred_sb[t] = inputs.tile([P, D_MODEL], BF16, name="pred%d" % t)
-            nc.sync.dma_start(out=pred_sb[t][:], in_=pred_view[:, t, :])
-
-        def load_rneg(t):
-            rneg_sb[t] = inputs.tile([P, D_MODEL], BF16, name="rneg%d" % t)
-            nc.sync.dma_start(out=rneg_sb[t][:], in_=rneg_view[:, t, :])
-
         def load_rsom(first, count):
             tiles = inputs.tile([P, count, N_SOM], BF16, name="rsom%d" % first)
             nc.sync.dma_start(out=tiles[:], in_=rsom_view[:, first : first + count, :])
@@ -130,49 +118,50 @@ def tile_pecircuits_pb_kernel(
         def load_words(dst, src, h):
             nc.sync.dma_start(out=dst[:, half(h)].bitcast(I32), in_=src[:, half(h)])
 
-        load_x(0)
+        def load_tiles(held, view, name, first, count):
+            tiles = inputs.tile([P, count, D_MODEL], BF16, name="%s%d" % (name, first))
+            nc.sync.dma_start(out=tiles[:], in_=view[:, first : first + count, :])
+            for t in range(first, first + count):
+                held[t] = tiles[:, t - first, :]
+
+        load_tiles(x_sb, x_view, "x", 0, 1)
         load_first_stage_words(0)
         load_planes(FF, ff_plane_rows)
         load_first_stage_words(1)
-        load_x(1)
+        load_tiles(x_sb, x_view, "x", 1, 1)
         load_rsom(0, 2)
-        load_x(2)
-        load_prediction(0)
+        load_tiles(x_sb, x_view, "x", 2, 1)
+        load_tiles(pred_sb, pred_view, "pred", 0, 1)
         load_words(som_words, som_dram, 0)
         load_planes(INH, inh_plane_rows)
         load_words(inh_words, inh_dram, 0)
         load_words(som_words, som_dram, 1)
         load_planes(SOM, som_plane_rows)
         load_words(inh_words, inh_dram, 1)
-        load_prediction(1)
-        load_x(3)
-        load_rneg(0)
-        load_prediction(2)
+        load_tiles(pred_sb, pred_view, "pred", 1, 1)
+        load_tiles(x_sb, x_view, "x", 3, 1)
+        load_tiles(rneg_sb, rneg_view, "rneg", 0, 1)
+        load_tiles(pred_sb, pred_view, "pred", 2, 1)
         load_rsom(2, 6)
-        load_x(4)
-        load_rneg(1)
-        load_rneg(2)
-        load_prediction(3)
-        load_x(5)
-        load_rneg(3)
-        load_prediction(4)
-        load_x(6)
-        load_rneg(4)
-        load_prediction(5)
-        load_x(7)
-        load_rneg(5)
-        load_prediction(6)
-        load_rneg(6)
-        load_prediction(7)
-        load_rneg(7)
+        load_tiles(x_sb, x_view, "x", 4, 1)
+        load_tiles(rneg_sb, rneg_view, "rneg", 1, 1)
+        load_tiles(x_sb, x_view, "x", 5, 1)
+        load_tiles(rneg_sb, rneg_view, "rneg", 2, 1)
+        load_tiles(pred_sb, pred_view, "pred", 3, 2)
+        load_tiles(x_sb, x_view, "x", 6, 2)
+        load_tiles(rneg_sb, rneg_view, "rneg", 3, 2)
+        load_tiles(pred_sb, pred_view, "pred", 5, 2)
+        load_tiles(rneg_sb, rneg_view, "rneg", 5, 2)
+        load_tiles(pred_sb, pred_view, "pred", 7, 1)
+        load_tiles(rneg_sb, rneg_view, "rneg", 7, 1)
 
         x_planes, x_grouped, x_codes, x_scales = {}, {}, {}, {}
         pv_sum, pv_sorted, act_planes, act_grouped, act_codes, act_scales = {}, {}, {}, {}, {}, {}
-        inhibition, error = {}, {}
+        inhibition, error, filtered = {}, {}, {}
         PV, SOM_ACT = 0, 1
 
         def transpose_x(t):
-            words = x_sb[t][:].bitcast(F32)
+            words = x_sb[t].bitcast(F32)
             for bank in range(2):
                 x_planes[t, bank] = psum.tile([P, 2, 2, P], F32, name="xT%d_%d" % (t, bank), tag="short", bufs=4)
                 for g2 in range(2):
@@ -307,11 +296,20 @@ def tile_pecircuits_pb_kernel(
             nc.scalar.activation(out=error_block(t, j), in_=error_block(t, j), func=ACT.Relu, scale=ALPHA)
 
         def filter_and_store(t, h):
-            filtered = work.tile([P, HALF], F32, name="out%d_%d" % (t, h), tag="out", bufs=OUT_BUFS)
+            if h == 0:
+                filtered[t] = work.tile([P, D_MODEL], F32, name="out%d" % t, tag="out", bufs=OUT_BUFS)
             nc.vector.scalar_tensor_tensor(
-                out=filtered[:], in0=rneg_sb[t][:, half(h)], scalar=1.0 - ALPHA, in1=error[t, h][:], op0=ALU.mult, op1=ALU.add
+                out=filtered[t][:, half(h)],
+                in0=rneg_sb[t][:, half(h)],
+                scalar=1.0 - ALPHA,
+                in1=error[t, h][:],
+                op0=ALU.mult,
+                op1=ALU.add,
             )
-            nc.sync.dma_start(out=out_view[:, t, half(h)], in_=filtered[:])
+            if t == TILES - 1:
+                nc.sync.dma_start(out=out_view[:, t, half(h)], in_=filtered[t][:, half(h)])
+            elif h == 1:
+                nc.sync.dma_start(out=out_view[:, t, :], in_=filtered[t][:])
 
         def live(t):
             return 0 <= t < TILES

@@ -157,7 +157,7 @@ def tile_pecircuits_pb_kernel(
 
         x_planes, x_grouped, x_codes, x_scales = {}, {}, {}, {}
         pv_sum, pv_sorted, act_planes, act_grouped, act_codes, act_scales = {}, {}, {}, {}, {}, {}
-        inhibition, error, filtered = {}, {}, {}
+        inhibition, error, filtered, scaled = {}, {}, {}, {}
         PV, SOM_ACT = 0, 1
 
         def transpose_x(t):
@@ -295,21 +295,31 @@ def tile_pecircuits_pb_kernel(
         def scaled_relu(t, j):
             nc.scalar.activation(out=error_block(t, j), in_=error_block(t, j), func=ACT.Relu, scale=ALPHA)
 
-        def filter_and_store(t, h):
-            if h == 0:
+        def store(t, cols):
+            nc.sync.dma_start(out=out_view[:, t, cols], in_=filtered[t][:, cols])
+
+        def filter_columns(t, first, count):
+            if first == 0:
                 filtered[t] = work.tile([P, D_MODEL], F32, name="out%d" % t, tag="out", bufs=OUT_BUFS)
+            start = (first * BANK) % HALF
+            cols = slice(first * BANK, (first + count) * BANK)
             nc.vector.scalar_tensor_tensor(
-                out=filtered[t][:, half(h)],
-                in0=rneg_sb[t][:, half(h)],
+                out=filtered[t][:, cols],
+                in0=rneg_sb[t][:, cols],
                 scalar=1.0 - ALPHA,
-                in1=error[t, h][:],
+                in1=error[t, first * BANK // HALF][:, start : start + count * BANK],
                 op0=ALU.mult,
                 op1=ALU.add,
             )
-            if t == TILES - 1:
-                nc.sync.dma_start(out=out_view[:, t, half(h)], in_=filtered[t][:, half(h)])
-            elif h == 1:
-                nc.sync.dma_start(out=out_view[:, t, :], in_=filtered[t][:])
+
+        def scale_rneg(t):
+            scaled[t] = work.tile([P, HALF], F32, name="scaled%d" % t, tag="scaled", bufs=1)
+            nc.scalar.activation(out=scaled[t][:], in_=rneg_sb[t][:, half(1)], func=ACT.Copy, scale=1.0 - ALPHA)
+
+        def filter_on_gpsimd(t):
+            for b in range(2):
+                cols = block(2 + b)
+                nc.gpsimd.tensor_tensor(out=filtered[t][:, cols], in0=scaled[t][:, b * BANK : (b + 1) * BANK], in1=error_block(t, 2 + b), op=ALU.add)
 
         def live(t):
             return 0 <= t < TILES
@@ -318,11 +328,18 @@ def tile_pecircuits_pb_kernel(
             if live(i):
                 quantise_activities(i)
             if live(i - 1):
-                filter_and_store(i - 1, 0)
+                filter_columns(i - 1, 0, 2)
+                if i - 1 >= TILES - 2:
+                    store(i - 1, half(0))
             if live(i + 2):
                 quantise_x(i + 2)
-            if live(i - 1):
-                filter_and_store(i - 1, 1)
+            if i - 1 == TILES - 1:
+                for b in range(2):
+                    filter_columns(i - 1, 2 + b, 1)
+                    store(i - 1, block(2 + b))
+            elif live(i - 1) and i - 1 != TILES - 2:
+                filter_columns(i - 1, 2, 2)
+                store(i - 1, slice(0, D_MODEL))
             if live(i + 1):
                 new_work(i + 1)
                 difference_on_vector(i + 1)
@@ -332,6 +349,9 @@ def tile_pecircuits_pb_kernel(
                 transpose_activities(i + 1)
                 group_activities(i + 1)
                 difference_on_gpsimd(i + 1)
+            if i == TILES - 1:
+                filter_on_gpsimd(i - 1)
+                store(i - 1, half(1))
             for j in range(BLOCKS):
                 if live(i):
                     subtract_inhibition(i, j)
@@ -344,3 +364,5 @@ def tile_pecircuits_pb_kernel(
                 relu_pv(i + 2)
             if live(i + 1):
                 difference_on_tensor(i + 1)
+            if i == TILES - 4:
+                scale_rneg(TILES - 2)

@@ -68,6 +68,8 @@ def tile_pecircuits_pb_kernel(
         FF, INH, SOM = 0, 1, 2
         planes = const.tile([P, 3, BANK], U8, align_bytes=64)
         nc.vector.memset(planes[:].rearrange("p w n -> p (w n)").bitcast(I32), 0)
+        idle_operand = const.tile([P, BANK], BF16)
+        nc.vector.memset(idle_operand[:], 0.0)
         minus_identity = const.tile([P, P], BF16)
         nc.vector.tensor_scalar_mul(minus_identity[:], plus_identity[:], -1.0)
 
@@ -129,14 +131,14 @@ def tile_pecircuits_pb_kernel(
         load_planes(FF, ff_plane_rows)
         load_first_stage_words(1)
         load_tiles(x_sb, x_view, "x", 1, 1)
+        load_planes(INH, inh_plane_rows)
         load_rsom(0, 2)
         load_tiles(x_sb, x_view, "x", 2, 1)
         load_tiles(pred_sb, pred_view, "pred", 0, 1)
+        load_planes(SOM, som_plane_rows)
         load_words(som_words, som_dram, 0)
-        load_planes(INH, inh_plane_rows)
         load_words(inh_words, inh_dram, 0)
         load_words(som_words, som_dram, 1)
-        load_planes(SOM, som_plane_rows)
         load_words(inh_words, inh_dram, 1)
         load_tiles(pred_sb, pred_view, "pred", 1, 1)
         load_tiles(x_sb, x_view, "x", 3, 1)
@@ -157,8 +159,13 @@ def tile_pecircuits_pb_kernel(
 
         x_planes, x_grouped, x_codes, x_scales = {}, {}, {}, {}
         pv_sum, pv_sorted, act_planes, act_grouped, act_codes, act_scales = {}, {}, {}, {}, {}, {}
-        inhibition, error, filtered, scaled = {}, {}, {}, {}
+        inhibition, error, filtered, diffs, scaled = {}, {}, {}, {}, {}
         PV, SOM_ACT = 0, 1
+
+        def keep_clock(count, tag="inh"):
+            unread = psum.tile([P, BANK], F32, name="unread", tag=tag, bufs=4)
+            for n in range(count):
+                nc.tensor.matmul(out=unread[:], lhsT=idle_operand[:, 0:P], rhs=idle_operand[:], start=True, stop=True)
 
         def transpose_x(t):
             words = x_sb[t].bitcast(F32)
@@ -236,8 +243,8 @@ def tile_pecircuits_pb_kernel(
                 in_=act_grouped[t][:].rearrange("q a b k -> q (a b k)"),
             )
 
-        def second_products(t):
-            for j in range(BLOCKS):
+        def second_products(t, h):
+            for j in (2 * h, 2 * h + 1):
                 inhibition[t, j] = psum.tile([P, BANK], F32, name="inh%d_%d" % (t, j), tag="inh", bufs=4)
                 nc.tensor.matmul_mx(
                     out=inhibition[t, j][:],
@@ -269,16 +276,23 @@ def tile_pecircuits_pb_kernel(
             first = (j % 2) * BANK
             return error[t, j // 2][:, first : first + BANK]
 
-        def difference_on_tensor(t):
+        def tensor_differences(t):
             for j in range(SHARES[t][0]):
-                diff = psum.tile([P, BANK], F32, name="diff%d_%d" % (t, j), tag="short", bufs=4)
-                nc.tensor.matmul(out=diff[:], lhsT=plus_identity[:], rhs=pred_sb[t][:, block(j)], start=True, stop=False)
-                nc.tensor.matmul(out=diff[:], lhsT=minus_identity[:], rhs=x_sb[t][:, block(j)], start=False, stop=True)
-                nc.scalar.copy(out=error_block(t, j), in_=diff[:])
+                diffs[t, j] = psum.tile([P, BANK], F32, name="diff%d_%d" % (t, j), tag="short", bufs=4)
+                nc.tensor.matmul(out=diffs[t, j][:], lhsT=plus_identity[:], rhs=pred_sb[t][:, block(j)], start=True, stop=False)
+                nc.tensor.matmul(out=diffs[t, j][:], lhsT=minus_identity[:], rhs=x_sb[t][:, block(j)], start=False, stop=True)
+
+        def copy_differences(t):
+            for j in range(SHARES[t][0]):
+                nc.scalar.copy(out=error_block(t, j), in_=diffs[t, j][:])
 
         def difference_on_gpsimd(t):
-            for j in range(BLOCKS - SHARES[t][1], BLOCKS):
-                nc.gpsimd.tensor_tensor(out=error_block(t, j), in0=pred_sb[t][:, block(j)], in1=x_sb[t][:, block(j)], op=ALU.subtract)
+            first = BLOCKS - SHARES[t][1]
+            if first < BLOCKS:
+                cols = slice(first * BANK, D_MODEL)
+                nc.gpsimd.tensor_tensor(
+                    out=error[t, 1][:, first * BANK - HALF :], in0=pred_sb[t][:, cols], in1=x_sb[t][:, cols], op=ALU.subtract
+                )
 
         def difference_on_vector(t):
             first, last = SHARES[t][0], BLOCKS - SHARES[t][1]
@@ -317,14 +331,14 @@ def tile_pecircuits_pb_kernel(
             nc.scalar.activation(out=scaled[t][:], in_=rneg_sb[t][:, half(1)], func=ACT.Copy, scale=1.0 - ALPHA)
 
         def filter_on_gpsimd(t):
-            for b in range(2):
-                cols = block(2 + b)
-                nc.gpsimd.tensor_tensor(out=filtered[t][:, cols], in0=scaled[t][:, b * BANK : (b + 1) * BANK], in1=error_block(t, 2 + b), op=ALU.add)
+            nc.gpsimd.tensor_tensor(out=filtered[t][:, half(1)], in0=scaled[t][:], in1=error[t, 1][:], op=ALU.add)
 
         def live(t):
             return 0 <= t < TILES
 
         for i in range(-3, TILES + 1):
+            if i == -3:
+                keep_clock(4)
             if live(i):
                 quantise_activities(i)
             if live(i - 1):
@@ -344,11 +358,19 @@ def tile_pecircuits_pb_kernel(
                 new_work(i + 1)
                 difference_on_vector(i + 1)
             if live(i):
-                second_products(i)
+                second_products(i, 0)
+                second_products(i, 1)
             if live(i + 1):
                 transpose_activities(i + 1)
                 group_activities(i + 1)
                 difference_on_gpsimd(i + 1)
+            if i < 0 and live(i + 2):
+                if i == -2:
+                    keep_clock(4)
+                if i == -1:
+                    keep_clock(3)
+                first_product(i + 2)
+                relu_pv(i + 2)
             if i == TILES - 1:
                 filter_on_gpsimd(i - 1)
                 store(i - 1, half(1))
@@ -359,10 +381,11 @@ def tile_pecircuits_pb_kernel(
                 if j == 1 and live(i + 3):
                     transpose_x(i + 3)
                     group_x(i + 3)
-            if live(i + 2):
+            if i >= 0 and live(i + 2):
                 first_product(i + 2)
                 relu_pv(i + 2)
             if live(i + 1):
-                difference_on_tensor(i + 1)
+                tensor_differences(i + 1)
+                copy_differences(i + 1)
             if i == TILES - 4:
                 scale_rneg(TILES - 2)

@@ -22,7 +22,7 @@ BANK = 512
 BLOCKS = D_MODEL // BANK
 HALF = D_MODEL // 2
 ALPHA = 0.1
-SHARES = [(0, 0)] + [(1, 2), (2, 2)] * 3 + [(2, 2)]
+SHARES = [(0, 0), (1, 1)] + [(1, 2), (2, 2)] * 3
 ERR_BUFS = 2
 OUT_BUFS = 6
 
@@ -143,11 +143,12 @@ def tile_pecircuits_pb_kernel(
         load_tiles(pred_sb, pred_view, "pred", 1, 1)
         load_tiles(x_sb, x_view, "x", 3, 1)
         load_tiles(rneg_sb, rneg_view, "rneg", 0, 1)
-        load_tiles(pred_sb, pred_view, "pred", 2, 1)
-        load_rsom(2, 6)
+        load_rsom(2, 2)
         load_tiles(x_sb, x_view, "x", 4, 1)
+        load_tiles(pred_sb, pred_view, "pred", 2, 1)
         load_tiles(rneg_sb, rneg_view, "rneg", 1, 1)
         load_tiles(x_sb, x_view, "x", 5, 1)
+        load_rsom(4, 4)
         load_tiles(rneg_sb, rneg_view, "rneg", 2, 1)
         load_tiles(pred_sb, pred_view, "pred", 3, 2)
         load_tiles(x_sb, x_view, "x", 6, 2)
@@ -288,11 +289,13 @@ def tile_pecircuits_pb_kernel(
 
         def difference_on_gpsimd(t):
             first = BLOCKS - SHARES[t][1]
-            if first < BLOCKS:
-                cols = slice(first * BANK, D_MODEL)
-                nc.gpsimd.tensor_tensor(
-                    out=error[t, 1][:, first * BANK - HALF :], in0=pred_sb[t][:, cols], in1=x_sb[t][:, cols], op=ALU.subtract
-                )
+            for h in range(2):
+                start = max(first * BANK - h * HALF, 0)
+                if start < HALF:
+                    cols = slice(h * HALF + start, (h + 1) * HALF)
+                    nc.gpsimd.tensor_tensor(
+                        out=error[t, h][:, start:], in0=pred_sb[t][:, cols], in1=x_sb[t][:, cols], op=ALU.subtract
+                    )
 
         def difference_on_vector(t):
             first, last = SHARES[t][0], BLOCKS - SHARES[t][1]
@@ -312,16 +315,15 @@ def tile_pecircuits_pb_kernel(
         def store(t, cols):
             nc.sync.dma_start(out=out_view[:, t, cols], in_=filtered[t][:, cols])
 
-        def filter_columns(t, first, count):
-            if first == 0:
+        def filter_columns(t, start, count):
+            if start == 0:
                 filtered[t] = work.tile([P, D_MODEL], F32, name="out%d" % t, tag="out", bufs=OUT_BUFS)
-            start = (first * BANK) % HALF
-            cols = slice(first * BANK, (first + count) * BANK)
+            cols = slice(start, start + count)
             nc.vector.scalar_tensor_tensor(
                 out=filtered[t][:, cols],
                 in0=rneg_sb[t][:, cols],
                 scalar=1.0 - ALPHA,
-                in1=error[t, first * BANK // HALF][:, start : start + count * BANK],
+                in1=error[t, start // HALF][:, start % HALF : start % HALF + count],
                 op0=ALU.mult,
                 op1=ALU.add,
             )
@@ -339,38 +341,49 @@ def tile_pecircuits_pb_kernel(
         for i in range(-3, TILES + 1):
             if i == -3:
                 keep_clock(4)
-            if live(i):
+            if live(i) and i != 1:
                 quantise_activities(i)
-            if live(i - 1):
-                filter_columns(i - 1, 0, 2)
-                if i - 1 >= TILES - 2:
+            if i - 1 == TILES - 1:
+                start = 0
+                for count in (BANK, BANK, BANK, BANK):
+                    filter_columns(i - 1, start, count)
+                    store(i - 1, slice(start, start + count))
+                    start += count
+            elif live(i - 1):
+                filter_columns(i - 1, 0, HALF)
+                if i - 1 == TILES - 2:
                     store(i - 1, half(0))
             if live(i + 2):
                 quantise_x(i + 2)
-            if i - 1 == TILES - 1:
-                for b in range(2):
-                    filter_columns(i - 1, 2 + b, 1)
-                    store(i - 1, block(2 + b))
-            elif live(i - 1) and i - 1 != TILES - 2:
-                filter_columns(i - 1, 2, 2)
+            if live(i - 1) and i - 1 < TILES - 2:
+                filter_columns(i - 1, HALF, HALF)
                 store(i - 1, slice(0, D_MODEL))
             if live(i + 1):
                 new_work(i + 1)
-                difference_on_vector(i + 1)
+                if i != 0:
+                    difference_on_vector(i + 1)
+            if i == 0:
+                transpose_activities(1)
+                group_activities(1)
             if live(i):
                 second_products(i, 0)
                 second_products(i, 1)
             if live(i + 1):
-                transpose_activities(i + 1)
-                group_activities(i + 1)
-                difference_on_gpsimd(i + 1)
-            if i < 0 and live(i + 2):
+                if i != 0:
+                    transpose_activities(i + 1)
+                    group_activities(i + 1)
+                else:
+                    quantise_activities(1)
+                if i != 0:
+                    difference_on_gpsimd(i + 1)
+            if i <= 0 and live(i + 2):
                 if i == -2:
                     keep_clock(4)
                 if i == -1:
                     keep_clock(3)
                 first_product(i + 2)
-                relu_pv(i + 2)
+                if i < 0:
+                    relu_pv(i + 2)
             if i == TILES - 1:
                 filter_on_gpsimd(i - 1)
                 store(i - 1, half(1))
@@ -378,10 +391,14 @@ def tile_pecircuits_pb_kernel(
                 if live(i):
                     subtract_inhibition(i, j)
                     scaled_relu(i, j)
-                if j == 1 and live(i + 3):
+                if j == (3 if i == 0 else 1) and live(i + 3):
                     transpose_x(i + 3)
                     group_x(i + 3)
-            if i >= 0 and live(i + 2):
+            if i == 0:
+                relu_pv(2)
+                difference_on_vector(1)
+                difference_on_gpsimd(1)
+            if i > 0 and live(i + 2):
                 first_product(i + 2)
                 relu_pv(i + 2)
             if live(i + 1):

from contextlib import ExitStack

import concourse.mybir as mybir
from concourse.masks import make_identity

F32 = mybir.dt.float32
BF16 = mybir.dt.bfloat16
I32 = mybir.dt.int32
U32 = mybir.dt.uint32
U8 = mybir.dt.uint8
FP8X4 = mybir.dt.float8_e4m3fn_x4
ALU = mybir.AluOpType
ACT = mybir.ActivationFunctionType

P = 128
PACK = 4
K_PASS = P * PACK
BATCH, D_MODEL, N_PV, N_SOM = 1024, 2048, 512, 512
TILES = BATCH // P
FF_PASSES = D_MODEL // K_PASS
BANK = 512
BLOCKS = D_MODEL // BANK
HALF = D_MODEL // 2
ALPHA = 0.1
SHARES = [(0, 0), (1, 1)] + [(1, 2), (2, 2)] * 3
ERR_BUFS = 2
OUT_BUFS = 6

FLOPS = 2 * BATCH * (D_MODEL * N_PV + N_PV * D_MODEL + N_SOM * D_MODEL)


def tile_pecircuits_pb_kernel(
    tc,
    x_batch,
    predicted,
    r_som,
    r_neg_batch,
    w_ff_words,
    w_ff_scales,
    w_inh_words,
    w_inh_scales,
    w_som_words,
    w_som_scales,
    out,
):
    nc = tc.nc

    x_view = x_batch.rearrange("(p t) d -> p t d", t=TILES)
    pred_view = predicted.rearrange("(p t) d -> p t d", t=TILES)
    rneg_view = r_neg_batch.rearrange("(p t) d -> p t d", t=TILES)
    rsom_view = r_som.rearrange("(p t) k -> p t k", t=TILES)
    out_view = out.rearrange("(p t) d -> p t d", t=TILES)

    with ExitStack() as ctx:
        const = ctx.enter_context(tc.tile_pool(name="const", bufs=1))
        inputs = ctx.enter_context(tc.tile_pool(name="inputs", bufs=1))
        stage = ctx.enter_context(tc.tile_pool(name="stage", bufs=2))
        quant = ctx.enter_context(tc.tile_pool(name="quant", bufs=3))
        work = ctx.enter_context(tc.tile_pool(name="work", bufs=7))
        psum = ctx.enter_context(tc.psum_pool(name="psum", bufs=1))
        ctx.enter_context(tc.manual_schedule())

        identity = const.tile([P, P], F32)
        make_identity(nc, identity[:])
        plus_identity = const.tile([P, P], BF16)
        make_identity(nc, plus_identity[:])

        FF, INH, SOM = 0, 1, 2
        planes = const.tile([P, 3, BANK], U8, align_bytes=64)
        nc.vector.memset(planes[:].rearrange("p w n -> p (w n)").bitcast(I32), 0)
        idle_operand = const.tile([P, BANK], BF16)
        nc.vector.memset(idle_operand[:], 0.0)
        minus_identity = const.tile([P, P], BF16)
        nc.vector.tensor_scalar_mul(minus_identity[:], plus_identity[:], -1.0)

        def load_planes(slab, four_planes):
            for quadrant in range(4):
                nc.sync.dma_start(
                    out=planes[32 * quadrant : 32 * quadrant + 16, slab, :].bitcast(I32),
                    in_=four_planes(quadrant),
                )

        def ff_plane_rows(quadrant):
            return w_ff_scales[:, 4 * quadrant : 4 * quadrant + 4, :].bitcast(I32)

        def inh_plane_rows(quadrant):
            rows = w_inh_scales[0, 4 * quadrant : 4 * quadrant + 4, :].bitcast(I32)
            return rows.rearrange("r (j n) -> j r n", j=BLOCKS)

        def som_plane_rows(quadrant):
            rows = w_som_scales[0, 4 * quadrant : 4 * quadrant + 4, :].bitcast(I32)
            return rows.rearrange("r (j n) -> j r n", j=BLOCKS)

        ff_words = const.tile([P, FF_PASSES, N_PV], U32, align_bytes=64)
        inh_words = const.tile([P, D_MODEL], U32, align_bytes=64)
        som_words = const.tile([P, D_MODEL], U32, align_bytes=64)
        inh_dram = w_inh_words[0].rearrange("p n t -> p (n t)").bitcast(I32)
        som_dram = w_som_words[0].rearrange("p n t -> p (n t)").bitcast(I32)

        def block(j):
            return slice(j * BANK, (j + 1) * BANK)

        def half(h):
            return slice(h * HALF, (h + 1) * HALF)

        x_sb, pred_sb, rneg_sb, rsom_sb = {}, {}, {}, {}

        def load_rsom(first, count):
            tiles = inputs.tile([P, count, N_SOM], BF16, name="rsom%d" % first)
            nc.sync.dma_start(out=tiles[:], in_=rsom_view[:, first : first + count, :])
            for t in range(first, first + count):
                rsom_sb[t] = tiles[:, t - first, :]

        def load_first_stage_words(h):
            nc.sync.dma_start(
                out=ff_words[:, 2 * h : 2 * h + 2, :].bitcast(I32),
                in_=w_ff_words[2 * h : 2 * h + 2].rearrange("g p n t -> p g (n t)").bitcast(I32),
            )

        def load_words(dst, src, h):
            nc.sync.dma_start(out=dst[:, half(h)].bitcast(I32), in_=src[:, half(h)])

        def load_tiles(held, view, name, first, count):
            tiles = inputs.tile([P, count, D_MODEL], BF16, name="%s%d" % (name, first))
            nc.sync.dma_start(out=tiles[:], in_=view[:, first : first + count, :])
            for t in range(first, first + count):
                held[t] = tiles[:, t - first, :]

        load_tiles(x_sb, x_view, "x", 0, 1)
        load_first_stage_words(0)
        load_planes(FF, ff_plane_rows)
        load_first_stage_words(1)
        load_tiles(x_sb, x_view, "x", 1, 1)
        load_planes(INH, inh_plane_rows)
        load_rsom(0, 2)
        load_tiles(x_sb, x_view, "x", 2, 1)
        load_tiles(pred_sb, pred_view, "pred", 0, 1)
        load_planes(SOM, som_plane_rows)
        load_words(som_words, som_dram, 0)
        load_words(inh_words, inh_dram, 0)
        load_words(som_words, som_dram, 1)
        load_words(inh_words, inh_dram, 1)
        load_tiles(pred_sb, pred_view, "pred", 1, 1)
        load_tiles(x_sb, x_view, "x", 3, 1)
        load_tiles(rneg_sb, rneg_view, "rneg", 0, 1)
        load_rsom(2, 2)
        load_tiles(x_sb, x_view, "x", 4, 1)
        load_tiles(pred_sb, pred_view, "pred", 2, 1)
        load_tiles(rneg_sb, rneg_view, "rneg", 1, 1)
        load_tiles(x_sb, x_view, "x", 5, 1)
        load_rsom(4, 4)
        load_tiles(rneg_sb, rneg_view, "rneg", 2, 1)
        load_tiles(pred_sb, pred_view, "pred", 3, 2)
        load_tiles(x_sb, x_view, "x", 6, 2)
        load_tiles(rneg_sb, rneg_view, "rneg", 3, 2)
        load_tiles(pred_sb, pred_view, "pred", 5, 2)
        load_tiles(rneg_sb, rneg_view, "rneg", 5, 2)
        load_tiles(pred_sb, pred_view, "pred", 7, 1)
        load_tiles(rneg_sb, rneg_view, "rneg", 7, 1)

        x_planes, x_grouped, x_codes, x_scales = {}, {}, {}, {}
        pv_sum, pv_sorted, act_planes, act_grouped, act_codes, act_scales = {}, {}, {}, {}, {}, {}
        inhibition, error, filtered, diffs, scaled = {}, {}, {}, {}, {}
        PV, SOM_ACT = 0, 1

        def keep_clock(count, tag="inh"):
            unread = psum.tile([P, BANK], F32, name="unread", tag=tag, bufs=4)
            for n in range(count):
                nc.tensor.matmul(out=unread[:], lhsT=idle_operand[:, 0:P], rhs=idle_operand[:], start=True, stop=True)

        def transpose_x(t):
            words = x_sb[t].bitcast(F32)
            for bank in range(2):
                x_planes[t, bank] = psum.tile([P, 2, 2, P], F32, name="xT%d_%d" % (t, bank), tag="short", bufs=4)
                for g2 in range(2):
                    first = (2 * bank + g2) * (K_PASS // 2)
                    for u in range(2):
                        nc.tensor.transpose(
                            x_planes[t, bank][:, g2, u, :],
                            words[:, first + u : first + K_PASS // 2 : 2],
                            identity[:],
                        )

        def group_x(t):
            x_grouped[t] = stage.tile([P, FF_PASSES, P, PACK], BF16, name="xg%d" % t, tag="xg", bufs=3, align_bytes=64)
            for bank in range(2):
                nc.scalar.copy(
                    out=x_grouped[t][:, 2 * bank : 2 * bank + 2, :, :].bitcast(F32),
                    in_=x_planes[t, bank][:].rearrange("q g u b -> q g b u"),
                )

        def quantise_x(t):
            x_codes[t] = quant.tile([P, FF_PASSES, P], U32, name="xc%d" % t, tag="xc", align_bytes=64)
            x_scales[t] = quant.tile([P, FF_PASSES, P], U8, name="xs%d" % t, tag="xs", align_bytes=64)
            nc.vector.quantize_mx(
                out=x_codes[t][:].rearrange("q g b -> q (g b)").bitcast(FP8X4),
                scales=x_scales[t][:].rearrange("q g b -> q (g b)"),
                in_=x_grouped[t][:].rearrange("q g b k -> q (g b k)"),
            )

        def first_product(t):
            pv_sum[t] = psum.tile([P, N_PV], F32, name="pv%d" % t, tag="short", bufs=4)
            for g in range(FF_PASSES):
                nc.tensor.matmul_mx(
                    out=pv_sum[t][:],
                    lhsT=x_codes[t][:, g, :].bitcast(FP8X4),
                    lhsT_scale=x_scales[t][:, g, :],
                    rhs=ff_words[:, g, :].bitcast(FP8X4),
                    rhs_scale=planes[4 * g : P, FF, :],
                    start=(g == 0),
                    stop=(g == FF_PASSES - 1),
                )

        def relu_pv(t):
            pv_sorted[t] = stage.tile([P, 2, P, 2], BF16, name="pvs%d" % t, tag="pvs")
            nc.scalar.activation(
                out=pv_sorted[t][:],
                in_=pv_sum[t][:].rearrange("b (q u e) -> b u q e", u=2, e=2),
                func=ACT.Relu,
            )

        def transpose_activities(t):
            act_planes[t] = psum.tile([P, 2, 2, P], F32, name="aT%d" % t, tag="short", bufs=4)
            pv_words = pv_sorted[t][:].rearrange("b u q e -> b (u q e)").bitcast(F32)
            som_act_words = rsom_sb[t].bitcast(F32)
            for u in range(2):
                nc.tensor.transpose(act_planes[t][:, PV, u, :], pv_words[:, u * P : (u + 1) * P], identity[:])
            for u in range(2):
                nc.tensor.transpose(act_planes[t][:, SOM_ACT, u, :], som_act_words[:, u : K_PASS // 2 : 2], identity[:])

        def group_activities(t):
            act_grouped[t] = stage.tile([P, 2, P, PACK], BF16, name="ag%d" % t, tag="ag", align_bytes=64)
            nc.scalar.copy(
                out=act_grouped[t][:].bitcast(F32),
                in_=act_planes[t][:].rearrange("q a u b -> q a b u"),
            )

        def quantise_activities(t):
            act_codes[t] = quant.tile([P, 2, P], U32, name="ac%d" % t, tag="ac", align_bytes=64)
            act_scales[t] = quant.tile([P, 2, P], U8, name="as%d" % t, tag="as", align_bytes=64)
            nc.vector.quantize_mx(
                out=act_codes[t][:].rearrange("q a b -> q (a b)").bitcast(FP8X4),
                scales=act_scales[t][:].rearrange("q a b -> q (a b)"),
                in_=act_grouped[t][:].rearrange("q a b k -> q (a b k)"),
            )

        def second_products(t, h):
            for j in (2 * h, 2 * h + 1):
                inhibition[t, j] = psum.tile([P, BANK], F32, name="inh%d_%d" % (t, j), tag="inh", bufs=4)
                nc.tensor.matmul_mx(
                    out=inhibition[t, j][:],
                    lhsT=act_codes[t][:, PV, :].bitcast(FP8X4),
                    lhsT_scale=act_scales[t][:, PV, :],
                    rhs=inh_words[:, block(j)].bitcast(FP8X4),
                    rhs_scale=planes[4 * j : P, INH, :],
                    start=True,
                    stop=False,
                )
                nc.tensor.matmul_mx(
                    out=inhibition[t, j][:],
                    lhsT=act_codes[t][:, SOM_ACT, :].bitcast(FP8X4),
                    lhsT_scale=act_scales[t][:, SOM_ACT, :],
                    rhs=som_words[:, block(j)].bitcast(FP8X4),
                    rhs_scale=planes[4 * j : P, SOM, :],
                    start=False,
                    stop=True,
                )

        def diff_shares(t):
            return SHARES[t]

        def new_work(t):
            for h in range(2):
                error[t, h] = work.tile([P, HALF], F32, name="err%d_%d" % (t, h), tag="err%d" % h, bufs=ERR_BUFS)

        def error_block(t, j):
            first = (j % 2) * BANK
            return error[t, j // 2][:, first : first + BANK]

        def tensor_differences(t):
            for j in range(SHARES[t][0]):
                diffs[t, j] = psum.tile([P, BANK], F32, name="diff%d_%d" % (t, j), tag="short", bufs=4)
                nc.tensor.matmul(out=diffs[t, j][:], lhsT=plus_identity[:], rhs=pred_sb[t][:, block(j)], start=True, stop=False)
                nc.tensor.matmul(out=diffs[t, j][:], lhsT=minus_identity[:], rhs=x_sb[t][:, block(j)], start=False, stop=True)

        def copy_differences(t):
            for j in range(SHARES[t][0]):
                nc.scalar.copy(out=error_block(t, j), in_=diffs[t, j][:])

        def difference_on_gpsimd(t):
            first = BLOCKS - SHARES[t][1]
            for h in range(2):
                start = max(first * BANK - h * HALF, 0)
                if start < HALF:
                    cols = slice(h * HALF + start, (h + 1) * HALF)
                    nc.gpsimd.tensor_tensor(
                        out=error[t, h][:, start:], in0=pred_sb[t][:, cols], in1=x_sb[t][:, cols], op=ALU.subtract
                    )

        def difference_on_vector(t):
            first, last = SHARES[t][0], BLOCKS - SHARES[t][1]
            if (first, last) == (0, BLOCKS):
                for h in range(2):
                    nc.vector.tensor_tensor(out=error[t, h][:], in0=pred_sb[t][:, half(h)], in1=x_sb[t][:, half(h)], op=ALU.subtract)
            else:
                for j in range(first, last):
                    nc.vector.tensor_tensor(out=error_block(t, j), in0=pred_sb[t][:, block(j)], in1=x_sb[t][:, block(j)], op=ALU.subtract)

        def subtract_inhibition(t, j):
            nc.vector.tensor_tensor(out=error_block(t, j), in0=error_block(t, j), in1=inhibition[t, j][:], op=ALU.subtract)

        def scaled_relu(t, j):
            nc.scalar.activation(out=error_block(t, j), in_=error_block(t, j), func=ACT.Relu, scale=ALPHA)

        def store(t, cols):
            nc.sync.dma_start(out=out_view[:, t, cols], in_=filtered[t][:, cols])

        def filter_columns(t, start, count):
            if start == 0:
                filtered[t] = work.tile([P, D_MODEL], F32, name="out%d" % t, tag="out", bufs=OUT_BUFS)
            cols = slice(start, start + count)
            nc.vector.scalar_tensor_tensor(
                out=filtered[t][:, cols],
                in0=rneg_sb[t][:, cols],
                scalar=1.0 - ALPHA,
                in1=error[t, start // HALF][:, start % HALF : start % HALF + count],
                op0=ALU.mult,
                op1=ALU.add,
            )

        def scale_rneg(t):
            scaled[t] = work.tile([P, HALF], F32, name="scaled%d" % t, tag="scaled", bufs=1)
            nc.scalar.activation(out=scaled[t][:], in_=rneg_sb[t][:, half(1)], func=ACT.Copy, scale=1.0 - ALPHA)

        def filter_on_gpsimd(t):
            nc.gpsimd.tensor_tensor(out=filtered[t][:, half(1)], in0=scaled[t][:], in1=error[t, 1][:], op=ALU.add)

        def live(t):
            return 0 <= t < TILES

        for i in range(-3, TILES + 1):
            if i == -3:
                keep_clock(4)
            if live(i) and i != 1:
                quantise_activities(i)
            if i - 1 == TILES - 1:
                start = 0
                for count in (BANK, BANK, BANK, BANK):
                    filter_columns(i - 1, start, count)
                    store(i - 1, slice(start, start + count))
                    start += count
            elif live(i - 1):
                filter_columns(i - 1, 0, HALF)
                if i - 1 == TILES - 2:
                    store(i - 1, half(0))
            if live(i + 2):
                quantise_x(i + 2)
            if live(i - 1) and i - 1 < TILES - 2:
                filter_columns(i - 1, HALF, HALF)
                store(i - 1, slice(0, D_MODEL))
            if live(i + 1):
                new_work(i + 1)
                if i != 0:
                    difference_on_vector(i + 1)
            if i == 0:
                transpose_activities(1)
                group_activities(1)
            if live(i):
                second_products(i, 0)
                second_products(i, 1)
            if live(i + 1):
                if i != 0:
                    transpose_activities(i + 1)
                    group_activities(i + 1)
                else:
                    quantise_activities(1)
                if i != 0:
                    difference_on_gpsimd(i + 1)
            if i <= 0 and live(i + 2):
                if i == -2:
                    keep_clock(4)
                if i == -1:
                    keep_clock(3)
                first_product(i + 2)
                if i < 0:
                    relu_pv(i + 2)
            if i == TILES - 1:
                filter_on_gpsimd(i - 1)
                store(i - 1, half(1))
            for j in range(BLOCKS):
                if live(i):
                    subtract_inhibition(i, j)
                    scaled_relu(i, j)
                if j == (3 if i == 0 else 1) and live(i + 3):
                    transpose_x(i + 3)
                    group_x(i + 3)
            if i == 0:
                relu_pv(2)
                difference_on_vector(1)
                difference_on_gpsimd(1)
            if i > 0 and live(i + 2):
                first_product(i + 2)
                relu_pv(i + 2)
            if live(i + 1):
                tensor_differences(i + 1)
                copy_differences(i + 1)
            if i == TILES - 4:
                scale_rneg(TILES - 2)
